import numpy as np
import ml_dtypes


def mxq(x, axis, fmt="e4m3"):
    dtype, down = {"e4m3": (ml_dtypes.float8_e4m3fn, 7), "e5m2": (ml_dtypes.float8_e5m2, 14)}[fmt]
    v = np.moveaxis(np.asarray(x, np.float32).astype(ml_dtypes.bfloat16).astype(np.float64), axis, -1)
    blocks = v.reshape(v.shape[:-1] + (-1, 32))
    amax = np.abs(blocks).max(-1, keepdims=True)
    byte = np.maximum(np.where(amax > 0, np.frexp(amax)[1] - 1 + 127, 0) - down, 1)
    scale = np.exp2(byte - 127.0)
    codes = (blocks / scale).astype(np.float32).astype(dtype).astype(np.float64)
    return np.moveaxis((codes * scale).reshape(v.shape), -1, axis)


WIDE = False


def mx_kscale(k):
    if not WIDE:
        return np.ones(k)
    levels = np.array([10, -10, 5, -5, 0])
    a = np.random.permutation(np.resize(levels, k // 512 * 4)).reshape(k // 512, 4)
    idx = np.arange(k)
    return np.exp2(a[idx // 512, idx % 128 // 32])


BF16 = ml_dtypes.bfloat16


def bf(x):
    return np.asarray(x, np.float32).astype(BF16)


def f64(x):
    return np.asarray(x).astype(np.float64)


E2M1 = np.array([0.0, 0.5, 1.0, 1.5, 2.0, 3.0, 4.0, 6.0, -0.0, -0.5, -1.0, -1.5, -2.0, -3.0, -4.0, -6.0])


def pack_weight(w, fmt):
    k, n = w.shape
    w = f64(bf(w)).reshape(k // 32, 32, n)
    amax = np.abs(w).max(1)
    if fmt == "e4m3":
        byte = np.frexp(amax)[1] - 1 + 127 - 7
    else:
        mant, ex = np.frexp(amax / 6.0)
        byte = np.where(mant > 0.5, ex, ex - 1) + 127
    byte = np.clip(np.where(amax > 0, byte, 1), 1, 254)
    scaled = (w * np.exp2(127.0 - byte)[:, None, :]).reshape(k, n).astype(np.float32)
    by_word = np.ascontiguousarray(scaled.reshape(k // 512, 128, 4, n).transpose(0, 1, 3, 2))
    if fmt == "e4m3":
        words = by_word.astype(ml_dtypes.float8_e4m3fn).view(np.uint8)
    else:
        c = by_word.astype(ml_dtypes.float4_e2m1fn).view(np.uint8) & 0xF
        words = c[..., 0::2] | (c[..., 1::2] << 4)
    return np.ascontiguousarray(words), np.ascontiguousarray(byte.astype(np.uint8).reshape(k // 512, 16, n))


def unpack_weight(words, scales, fmt):
    g, p, n, _ = words.shape
    if fmt == "e4m3":
        vals = np.ascontiguousarray(words).view(ml_dtypes.float8_e4m3fn).astype(np.float64)
    else:
        nib = np.empty((g, p, n, 4), np.uint8)
        nib[..., 0::2] = words & 0xF
        nib[..., 1::2] = words >> 4
        vals = E2M1[nib]
    vals = vals * np.repeat(np.exp2(scales.astype(np.float64) - 127.0), 8, axis=1)[..., None]
    return vals.transpose(0, 1, 3, 2).reshape(g * 512, n)


B, D, H, O = 2048, 512, 512, 512


def silu(v):
    with np.errstate(over="ignore"):
        return v / (1.0 + np.exp(-v))


def setup_inputs():
    s = mx_kscale(H)
    u = s / s.min()
    t = bf(np.random.random(B))
    W1_words, W1_scales = pack_weight(np.ascontiguousarray((np.random.standard_normal((H, D)) * 2.0 / np.sqrt(D) * u[:, None]).T), "e4m3")
    b1 = bf(np.random.standard_normal(H) * 0.5 * u)
    W2_words, W2_scales = pack_weight(np.ascontiguousarray((np.random.standard_normal((O, H)) * 1.5 / np.sqrt(H) / u[None, :]).T), "e4m3")
    b2 = bf(np.random.standard_normal(O) * 0.5)
    return {"t": t,
            "W1_words": W1_words,
            "W1_scales": W1_scales,
            "b1": b1,
            "W2_words": W2_words,
            "W2_scales": W2_scales,
            "b2": b2}


def reference(t, W1_words, W1_scales, b1, W2_words, W2_scales, b2):
    t = f64(t)
    phase = (np.arange(D, dtype=np.float64) / D) * np.pi
    tb = t[:, None]
    emb = tb * np.cos(phase[None, :] * tb) + tb * np.sin(phase[None, :] * (1.0 - tb))
    x = silu((mxq(emb, 1, "e4m3") @ unpack_weight(W1_words, W1_scales, "e4m3")) + f64(b1))
    x = silu((mxq(x, 1, "e4m3") @ unpack_weight(W2_words, W2_scales, "e4m3")) + f64(b2))
    return x

@@ -1,0 +1,225 @@
+import math
+from contextlib import ExitStack
+
+import concourse.mybir as mybir
+from concourse.masks import make_identity
+
+F32 = mybir.dt.float32
+BF16 = mybir.dt.bfloat16
+I32 = mybir.dt.int32
+U32 = mybir.dt.uint32
+U8 = mybir.dt.uint8
+FP8X4 = mybir.dt.float8_e4m3fn_x4
+ACT = mybir.ActivationFunctionType
+ALU = mybir.AluOpType
+
+P = 128
+PACK = 4
+B, D, H, O = 2048, 512, 512, 512
+CHUNK = 512
+CHUNKS = B // CHUNK
+BLOCKS_PER_CHUNK = CHUNK // P
+VECTOR_COLS = 256
+RUN = 4
+
+FLOPS = 2 * B * (D * H + H * O)
+
+
+def tile_input_timestep_kernel(tc, t, W1_words, W1_scales, b1, W2_words, W2_scales, b2, out):
+    nc = tc.nc
+    with ExitStack() as ctx:
+        keep = ctx.enter_context(tc.tile_pool(name="keep", bufs=1))
+        work = ctx.enter_context(tc.tile_pool(name="work", bufs=4))
+        psum_acc = ctx.enter_context(tc.psum_pool(name="psum_acc", bufs=4))
+        psum_t = ctx.enter_context(tc.psum_pool(name="psum_t", bufs=4))
+        ctx.enter_context(tc.manual_schedule())
+
+        t_all = keep.tile([P, B], BF16)
+        for c in range(CHUNKS):
+            cols = slice(c * CHUNK, (c + 1) * CHUNK)
+            nc.sync.dma_start(out=t_all[:, cols], in_=t[cols].partition_broadcast(P))
+
+        w_scales = keep.tile([P, 2, H], U8, align_bytes=64)
+        nc.vector.memset(w_scales[:].rearrange("p w n -> p (w n)").bitcast(I32), 0)
+        w_words = keep.tile([P, 2, PACK * H], U8, align_bytes=64)
+        b1_all = keep.tile([P, H], BF16)
+        b2_all = keep.tile([P, O], BF16)
+        for w, (words, scales, bias, bias_all) in enumerate(
+            ((W1_words, W1_scales, b1, b1_all), (W2_words, W2_scales, b2, b2_all))
+        ):
+            for q in range(4):
+                nc.sync.dma_start(
+                    out=w_scales[32 * q : 32 * q + 4, w, :].bitcast(I32),
+                    in_=scales[0, 4 * q : 4 * q + 4, :].bitcast(I32),
+                )
+            nc.sync.dma_start(
+                out=w_words[:, w, :].bitcast(I32),
+                in_=words[0].rearrange("p n j -> p (n j)").bitcast(I32),
+            )
+            nc.sync.dma_start(out=bias_all[:], in_=bias.partition_broadcast(P))
+
+        k_int = keep.tile([P, PACK], I32)
+        nc.gpsimd.iota(k_int[:], pattern=[[1, PACK]], base=0, channel_multiplier=PACK)
+        k_f32 = keep.tile([P, PACK], F32)
+        nc.vector.tensor_copy(out=k_f32[:], in_=k_int[:])
+        neg_phase = keep.tile([P, PACK], F32)
+        nc.vector.tensor_scalar(out=neg_phase[:], in0=k_f32[:], scalar1=-math.pi / D, scalar2=None, op0=ALU.mult)
+        shift = keep.tile([P, PACK], F32)
+        nc.vector.tensor_scalar(
+            out=shift[:], in0=k_f32[:], scalar1=math.pi / (2 * D), scalar2=math.pi / 4, op0=ALU.mult, op1=ALU.add
+        )
+        sin_shift = keep.tile([P, PACK], F32)
+        nc.scalar.activation(out=sin_shift[:], in_=shift[:], func=ACT.Sin)
+        amplitude = keep.tile([P, PACK], F32)
+        nc.vector.tensor_scalar(out=amplitude[:], in0=sin_shift[:], scalar1=2.0, scalar2=None, op0=ALU.mult)
+
+        identity = keep.tile([P, P], F32)
+        make_identity(nc, identity[:])
+
+        sines = keep.tile([P, PACK, B], F32)
+        emb_rows = keep.tile([P, PACK, B], BF16)
+        emb_grouped = keep.tile([P, B, PACK], BF16, align_bytes=64)
+        emb_codes = keep.tile([P, B], U32, align_bytes=64)
+        emb_scales = keep.tile([P, B], U8, align_bytes=64)
+        b1_sorted = keep.tile([P, PACK, P], F32)
+        h_grouped = keep.tile([P, B, PACK], BF16, align_bytes=64)
+        h_codes = keep.tile([P, B], U32, align_bytes=64)
+        h_scales = keep.tile([P, B], U8, align_bytes=64)
+        acc_1 = {}
+        pre_1T = {}
+        acc_2 = {}
+
+        def blocks_of(c):
+            return range(c * BLOCKS_PER_CHUNK, (c + 1) * BLOCKS_PER_CHUNK)
+
+        def sines_of(c):
+            cols = slice(c * CHUNK, (c + 1) * CHUNK)
+            for j in range(PACK):
+                nc.scalar.activation(
+                    out=sines[:, j, cols],
+                    in_=t_all[:, cols],
+                    func=ACT.Sin,
+                    bias=shift[:, j : j + 1],
+                    scale=neg_phase[:, j : j + 1],
+                )
+
+        def scale_by_t(c):
+            cols = slice(c * CHUNK, (c + 1) * CHUNK)
+            for j in range(PACK):
+                nc.vector.scalar_tensor_tensor(
+                    out=emb_rows[:, j, cols],
+                    in0=sines[:, j, cols],
+                    scalar=amplitude[:, j : j + 1],
+                    in1=t_all[:, cols],
+                    op0=ALU.mult,
+                    op1=ALU.mult,
+                )
+
+        def regroup(c):
+            split = c * CHUNK + VECTOR_COLS
+            for copy, cols in (
+                (nc.vector.tensor_copy, slice(c * CHUNK, split)),
+                (nc.scalar.copy, slice(split, (c + 1) * CHUNK)),
+            ):
+                copy(
+                    out=emb_grouped[:, cols, :].rearrange("p (g i) j -> p g j i", i=RUN),
+                    in_=emb_rows[:, :, cols].rearrange("p j (g i) -> p g j i", i=RUN),
+                )
+
+        def quantise_emb(c):
+            cols = slice(c * CHUNK, (c + 1) * CHUNK)
+            nc.vector.quantize_mx(
+                out=emb_codes[:, cols].bitcast(FP8X4),
+                scales=emb_scales[:, cols],
+                in_=emb_grouped[:, cols, :].rearrange("p b j -> p (b j)"),
+            )
+
+        def layer1_matmuls(c):
+            for i in blocks_of(c):
+                rows = slice(i * P, (i + 1) * P)
+                acc_1[i] = psum_acc.tile([P, H], F32, name="acc_1", tag="acc")
+                nc.tensor.matmul_mx(
+                    out=acc_1[i][:],
+                    lhsT=emb_codes[:, rows].bitcast(FP8X4),
+                    lhsT_scale=emb_scales[:, rows],
+                    rhs=w_words[:, 0, :].bitcast(FP8X4),
+                    rhs_scale=w_scales[:, 0, :],
+                    start=True,
+                    stop=True,
+                )
+
+        def layer1_bias_and_transpose(c):
+            for i in blocks_of(c):
+                pre_1 = work.tile([P, PACK, P], F32)
+                nc.vector.tensor_tensor(
+                    out=pre_1[:], in0=acc_1[i][:].rearrange("b (p j) -> b j p", j=PACK), in1=b1_sorted[:], op=ALU.add
+                )
+                pre_1T[i] = psum_t.tile([P, PACK, P], F32, name="pre_1T")
+                for j in range(PACK):
+                    nc.tensor.transpose(pre_1T[i][:, j, :], pre_1[:, j, :], identity[:])
+
+        def layer1_silu(c):
+            for i in blocks_of(c):
+                rows = slice(i * P, (i + 1) * P)
+                nc.scalar.activation(
+                    out=h_grouped[:, rows, :], in_=pre_1T[i][:].rearrange("p j b -> p b j"), func=ACT.Silu
+                )
+
+        def quantise_h(c):
+            for i in blocks_of(c):
+                rows = slice(i * P, (i + 1) * P)
+                nc.vector.quantize_mx(
+                    out=h_codes[:, rows].bitcast(FP8X4),
+                    scales=h_scales[:, rows],
+                    in_=h_grouped[:, rows, :].rearrange("p b j -> p (b j)"),
+                )
+
+        def layer2_matmuls(c):
+            for i in blocks_of(c):
+                rows = slice(i * P, (i + 1) * P)
+                acc_2[i] = psum_acc.tile([P, O], F32, name="acc_2", tag="acc")
+                nc.tensor.matmul_mx(
+                    out=acc_2[i][:],
+                    lhsT=h_codes[:, rows].bitcast(FP8X4),
+                    lhsT_scale=h_scales[:, rows],
+                    rhs=w_words[:, 1, :].bitcast(FP8X4),
+                    rhs_scale=w_scales[:, 1, :],
+                    start=True,
+                    stop=True,
+                )
+
+        def layer2_finish(c):
+            for i in blocks_of(c):
+                rows = slice(i * P, (i + 1) * P)
+                pre_2 = work.tile([P, O], F32)
+                nc.vector.tensor_tensor(out=pre_2[:], in0=acc_2[i][:], in1=b2_all[:], op=ALU.add)
+                result = work.tile([P, O], F32)
+                nc.scalar.activation(out=result[:], in_=pre_2[:], func=ACT.Silu)
+                nc.sync.dma_start(out=out[rows, :], in_=result[:])
+
+        sines_of(0)
+        sines_of(1)
+        scale_by_t(0)
+        regroup(0)
+        sines_of(2)
+        scale_by_t(1)
+        regroup(1)
+        sines_of(3)
+        quantise_emb(0)
+        nc.vector.tensor_copy(out=b1_sorted[:], in_=b1_all[:].rearrange("b (p j) -> b j p", j=PACK))
+        layer1_matmuls(0)
+        for c in range(CHUNKS + 1):
+            if c < CHUNKS:
+                layer1_bias_and_transpose(c)
+                layer1_silu(c)
+            if c + 2 < CHUNKS:
+                scale_by_t(c + 2)
+                regroup(c + 2)
+            if c + 1 < CHUNKS:
+                quantise_emb(c + 1)
+            if c >= 1:
+                quantise_h(c - 1)
+                layer2_matmuls(c - 1)
+                layer2_finish(c - 1)
+            if c + 1 < CHUNKS:
+                layer1_matmuls(c + 1)

@@ -34,19 +34,16 @@ def tile_input_timestep_kernel(tc, t, W1_words, W1_scales, b1, W2_words, W2_scal
         psum_t = ctx.enter_context(tc.psum_pool(name="psum_t", bufs=4))
         ctx.enter_context(tc.manual_schedule())
 
-        t_all = keep.tile([P, B], BF16)
-        for c in range(CHUNKS):
-            cols = slice(c * CHUNK, (c + 1) * CHUNK)
-            nc.sync.dma_start(out=t_all[:, cols], in_=t[cols].partition_broadcast(P))
+        rows = keep.tile([P, B + H + O], BF16)
+        nc.vector.memset(rows[:].bitcast(I32), 0)
+        nc.sync.dma_start(out=rows[0:1, 0:B], in_=t.unsqueeze(0))
+        nc.sync.dma_start(out=rows[0:1, B : B + H], in_=b1.unsqueeze(0))
+        nc.sync.dma_start(out=rows[0:1, B + H : B + H + O], in_=b2.unsqueeze(0))
 
         w_scales = keep.tile([P, 2, H], U8, align_bytes=64)
         nc.vector.memset(w_scales[:].rearrange("p w n -> p (w n)").bitcast(I32), 0)
         w_words = keep.tile([P, 2, PACK * H], U8, align_bytes=64)
-        b1_all = keep.tile([P, H], BF16)
-        b2_all = keep.tile([P, O], BF16)
-        for w, (words, scales, bias, bias_all) in enumerate(
-            ((W1_words, W1_scales, b1, b1_all), (W2_words, W2_scales, b2, b2_all))
-        ):
+        for w, (words, scales) in enumerate(((W1_words, W1_scales), (W2_words, W2_scales))):
             for q in range(4):
                 nc.sync.dma_start(
                     out=w_scales[32 * q : 32 * q + 4, w, :].bitcast(I32),
@@ -56,7 +53,22 @@ def tile_input_timestep_kernel(tc, t, W1_words, W1_scales, b1, W2_words, W2_scal
                 out=w_words[:, w, :].bitcast(I32),
                 in_=words[0].rearrange("p n j -> p (n j)").bitcast(I32),
             )
-            nc.sync.dma_start(out=bias_all[:], in_=bias.partition_broadcast(P))
+
+        ones = keep.tile([P, P], BF16)
+        nc.gpsimd.memset(ones[:], 1.0)
+        on_all = {}
+
+        def put_on_all(first):
+            on_all[first] = psum_acc.tile([P, CHUNK], F32, name="on_all", tag="acc")
+            nc.tensor.matmul(
+                out=on_all[first][:], lhsT=ones[:], rhs=rows[:, first : first + CHUNK], start=True, stop=True
+            )
+
+        t_all = keep.tile([P, B], BF16)
+        b2_all = keep.tile([P, O], F32)
+
+        def copy_t(c):
+            nc.vector.tensor_copy(out=t_all[:, c * CHUNK : (c + 1) * CHUNK], in_=on_all[c * CHUNK][:])
 
         k_int = keep.tile([P, PACK], I32)
         nc.gpsimd.iota(k_int[:], pattern=[[1, PACK]], base=0, channel_multiplier=PACK)
@@ -197,16 +209,25 @@ def tile_input_timestep_kernel(tc, t, W1_words, W1_scales, b1, W2_words, W2_scal
                 nc.scalar.activation(out=result[:], in_=pre_2[:], func=ACT.Silu)
                 nc.sync.dma_start(out=out[rows, :], in_=result[:])
 
+        for c in range(CHUNKS):
+            put_on_all(c * CHUNK)
+        copy_t(0)
+        copy_t(1)
+        put_on_all(B)
+        put_on_all(B + H)
         sines_of(0)
         sines_of(1)
         scale_by_t(0)
         regroup(0)
+        copy_t(2)
         sines_of(2)
         scale_by_t(1)
         regroup(1)
+        copy_t(3)
         sines_of(3)
         quantise_emb(0)
-        nc.vector.tensor_copy(out=b1_sorted[:], in_=b1_all[:].rearrange("b (p j) -> b j p", j=PACK))
+        nc.vector.tensor_copy(out=b1_sorted[:], in_=on_all[B][:].rearrange("b (p j) -> b j p", j=PACK))
+        nc.vector.tensor_copy(out=b2_all[:], in_=on_all[B + H][:])
         layer1_matmuls(0)
         for c in range(CHUNKS + 1):
             if c < CHUNKS:

@@ -35,10 +35,11 @@ def tile_input_timestep_kernel(tc, t, W1_words, W1_scales, b1, W2_words, W2_scal
         ctx.enter_context(tc.manual_schedule())
 
         rows = keep.tile([P, B + H + O], BF16)
-        nc.vector.memset(rows[:].bitcast(I32), 0)
-        nc.sync.dma_start(out=rows[0:1, 0:B], in_=t.unsqueeze(0))
-        nc.sync.dma_start(out=rows[0:1, B : B + H], in_=b1.unsqueeze(0))
-        nc.sync.dma_start(out=rows[0:1, B + H : B + H + O], in_=b2.unsqueeze(0))
+        pieces = [t[c * CHUNK : (c + 1) * CHUNK] for c in range(CHUNKS)] + [b1, b2]
+        for n, piece in enumerate(pieces):
+            cols = slice(n * CHUNK, (n + 1) * CHUNK)
+            nc.vector.memset(rows[:, cols].bitcast(I32), 0)
+            nc.sync.dma_start(out=rows[0:1, cols], in_=piece.unsqueeze(0))
 
         w_scales = keep.tile([P, 2, H], U8, align_bytes=64)
         nc.vector.memset(w_scales[:].rearrange("p w n -> p (w n)").bitcast(I32), 0)
@@ -59,13 +60,13 @@ def tile_input_timestep_kernel(tc, t, W1_words, W1_scales, b1, W2_words, W2_scal
         on_all = {}
 
         def put_on_all(first):
-            on_all[first] = psum_acc.tile([P, CHUNK], F32, name="on_all", tag="acc")
+            on_all[first] = psum_t.tile([P, CHUNK], BF16, name="on_all", tag="flipped")
             nc.tensor.matmul(
                 out=on_all[first][:], lhsT=ones[:], rhs=rows[:, first : first + CHUNK], start=True, stop=True
             )
 
         t_all = keep.tile([P, B], BF16)
-        b2_all = keep.tile([P, O], F32)
+        b2_all = keep.tile([P, O], BF16)
 
         def copy_t(c):
             nc.vector.tensor_copy(out=t_all[:, c * CHUNK : (c + 1) * CHUNK], in_=on_all[c * CHUNK][:])
@@ -166,7 +167,7 @@ def tile_input_timestep_kernel(tc, t, W1_words, W1_scales, b1, W2_words, W2_scal
                 nc.vector.tensor_tensor(
                     out=pre_1[:], in0=acc_1[i][:].rearrange("b (p j) -> b j p", j=PACK), in1=b1_sorted[:], op=ALU.add
                 )
-                pre_1T[i] = psum_t.tile([P, PACK, P], F32, name="pre_1T")
+                pre_1T[i] = psum_t.tile([P, PACK, P], F32, name="pre_1T", tag="flipped")
                 for j in range(PACK):
                     nc.tensor.transpose(pre_1T[i][:, j, :], pre_1[:, j, :], identity[:])
 
@@ -211,36 +212,35 @@ def tile_input_timestep_kernel(tc, t, W1_words, W1_scales, b1, W2_words, W2_scal
 
         for c in range(CHUNKS):
             put_on_all(c * CHUNK)
-        copy_t(0)
-        copy_t(1)
+        for c in range(CHUNKS):
+            copy_t(c)
         put_on_all(B)
         put_on_all(B + H)
         sines_of(0)
         sines_of(1)
         scale_by_t(0)
         regroup(0)
-        copy_t(2)
         sines_of(2)
         scale_by_t(1)
-        regroup(1)
-        copy_t(3)
-        sines_of(3)
         quantise_emb(0)
+        layer1_matmuls(0)
+        regroup(1)
+        sines_of(3)
         nc.vector.tensor_copy(out=b1_sorted[:], in_=on_all[B][:].rearrange("b (p j) -> b j p", j=PACK))
         nc.vector.tensor_copy(out=b2_all[:], in_=on_all[B + H][:])
-        layer1_matmuls(0)
         for c in range(CHUNKS + 1):
             if c < CHUNKS:
                 layer1_bias_and_transpose(c)
                 layer1_silu(c)
-            if c + 2 < CHUNKS:
-                scale_by_t(c + 2)
-                regroup(c + 2)
-            if c + 1 < CHUNKS:
-                quantise_emb(c + 1)
             if c >= 1:
                 quantise_h(c - 1)
                 layer2_matmuls(c - 1)
+            if c + 1 < CHUNKS:
+                quantise_emb(c + 1)
+            if c + 2 < CHUNKS:
+                scale_by_t(c + 2)
+                regroup(c + 2)
+            if c >= 1:
                 layer2_finish(c - 1)
             if c + 1 < CHUNKS:
                 layer1_matmuls(c + 1)

@@ -2,7 +2,6 @@ import math
 from contextlib import ExitStack
 
 import concourse.mybir as mybir
-from concourse.masks import make_identity
 
 F32 = mybir.dt.float32
 BF16 = mybir.dt.bfloat16
@@ -18,8 +17,7 @@ PACK = 4
 B, D, H, O = 2048, 512, 512, 512
 CHUNK = 512
 CHUNKS = B // CHUNK
-BLOCKS_PER_CHUNK = CHUNK // P
-VECTOR_COLS = 256
+STRIPS_PER_CHUNK = CHUNK // P
 RUN = 4
 
 FLOPS = 2 * B * (D * H + H * O)
@@ -29,21 +27,22 @@ def tile_input_timestep_kernel(tc, t, W1_words, W1_scales, b1, W2_words, W2_scal
     nc = tc.nc
     with ExitStack() as ctx:
         keep = ctx.enter_context(tc.tile_pool(name="keep", bufs=1))
-        work = ctx.enter_context(tc.tile_pool(name="work", bufs=4))
-        psum_acc = ctx.enter_context(tc.psum_pool(name="psum_acc", bufs=4))
-        psum_t = ctx.enter_context(tc.psum_pool(name="psum_t", bufs=4))
+        work = ctx.enter_context(tc.tile_pool(name="work", bufs=3))
+        psum_acc = ctx.enter_context(tc.psum_pool(name="psum_acc", bufs=6))
+        psum_t = ctx.enter_context(tc.psum_pool(name="psum_t", bufs=2))
         ctx.enter_context(tc.manual_schedule())
 
-        rows = keep.tile([P, B + H + O], BF16)
-        pieces = [t[c * CHUNK : (c + 1) * CHUNK] for c in range(CHUNKS)] + [b1, b2]
-        for n, piece in enumerate(pieces):
-            cols = slice(n * CHUNK, (n + 1) * CHUNK)
+        rows = keep.tile([P, B], BF16)
+        for c in range(CHUNKS):
+            cols = slice(c * CHUNK, (c + 1) * CHUNK)
             nc.vector.memset(rows[:, cols].bitcast(I32), 0)
-            nc.sync.dma_start(out=rows[0:1, cols], in_=piece.unsqueeze(0))
+            nc.sync.dma_start(out=rows[0:1, cols], in_=t[cols].unsqueeze(0))
 
         w_scales = keep.tile([P, 2, H], U8, align_bytes=64)
         nc.vector.memset(w_scales[:].rearrange("p w n -> p (w n)").bitcast(I32), 0)
         w_words = keep.tile([P, 2, PACK * H], U8, align_bytes=64)
+        b1_bf = keep.tile([P, PACK], BF16)
+        b2_all = keep.tile([P, O], BF16)
         for w, (words, scales) in enumerate(((W1_words, W1_scales), (W2_words, W2_scales))):
             for q in range(4):
                 nc.sync.dma_start(
@@ -54,22 +53,25 @@ def tile_input_timestep_kernel(tc, t, W1_words, W1_scales, b1, W2_words, W2_scal
                 out=w_words[:, w, :].bitcast(I32),
                 in_=words[0].rearrange("p n j -> p (n j)").bitcast(I32),
             )
+            if w == 0:
+                nc.sync.dma_start(out=b1_bf[:], in_=b1.rearrange("(p j) -> p j", j=PACK))
+        nc.sync.dma_start(out=b2_all[:], in_=b2.partition_broadcast(P))
 
         ones = keep.tile([P, P], BF16)
         nc.gpsimd.memset(ones[:], 1.0)
-        on_all = {}
-
-        def put_on_all(first):
-            on_all[first] = psum_t.tile([P, CHUNK], BF16, name="on_all", tag="flipped")
-            nc.tensor.matmul(
-                out=on_all[first][:], lhsT=ones[:], rhs=rows[:, first : first + CHUNK], start=True, stop=True
-            )
-
+        t_psum = {}
         t_all = keep.tile([P, B], BF16)
-        b2_all = keep.tile([P, O], BF16)
+
+        def t_of(c):
+            return t_psum[c // 2][:, (c % 2) * CHUNK : (c % 2 + 1) * CHUNK]
+
+        def spread_t(c):
+            if c % 2 == 0:
+                t_psum[c // 2] = psum_t.tile([P, 2 * CHUNK], BF16, name="t_psum", tag="t_psum")
+            nc.tensor.matmul(out=t_of(c), lhsT=ones[:], rhs=rows[:, c * CHUNK : (c + 1) * CHUNK], start=True, stop=True)
 
         def copy_t(c):
-            nc.vector.tensor_copy(out=t_all[:, c * CHUNK : (c + 1) * CHUNK], in_=on_all[c * CHUNK][:])
+            nc.vector.tensor_copy(out=t_all[:, c * CHUNK : (c + 1) * CHUNK], in_=t_of(c))
 
         k_int = keep.tile([P, PACK], I32)
         nc.gpsimd.iota(k_int[:], pattern=[[1, PACK]], base=0, channel_multiplier=PACK)
@@ -86,24 +88,21 @@ def tile_input_timestep_kernel(tc, t, W1_words, W1_scales, b1, W2_words, W2_scal
         amplitude = keep.tile([P, PACK], F32)
         nc.vector.tensor_scalar(out=amplitude[:], in0=sin_shift[:], scalar1=2.0, scalar2=None, op0=ALU.mult)
 
-        identity = keep.tile([P, P], F32)
-        make_identity(nc, identity[:])
-
         sines = keep.tile([P, PACK, B], F32)
         emb_rows = keep.tile([P, PACK, B], BF16)
-        emb_grouped = keep.tile([P, B, PACK], BF16, align_bytes=64)
+        emb_grouped = {}
         emb_codes = keep.tile([P, B], U32, align_bytes=64)
         emb_scales = keep.tile([P, B], U8, align_bytes=64)
-        b1_sorted = keep.tile([P, PACK, P], F32)
-        h_grouped = keep.tile([P, B, PACK], BF16, align_bytes=64)
+        w1_codes = keep.tile([P, H], I32, align_bytes=64)
+        w1_scales = keep.tile([P, H], U8, align_bytes=64)
+        b1_cols = keep.tile([P, PACK], F32)
+        h_rows = keep.tile([P, PACK, B], BF16)
+        h_grouped = {}
         h_codes = keep.tile([P, B], U32, align_bytes=64)
         h_scales = keep.tile([P, B], U8, align_bytes=64)
         acc_1 = {}
-        pre_1T = {}
         acc_2 = {}
-
-        def blocks_of(c):
-            return range(c * BLOCKS_PER_CHUNK, (c + 1) * BLOCKS_PER_CHUNK)
+        pre_2 = {}
 
         def sines_of(c):
             cols = slice(c * CHUNK, (c + 1) * CHUNK)
@@ -123,124 +122,151 @@ def tile_input_timestep_kernel(tc, t, W1_words, W1_scales, b1, W2_words, W2_scal
                     out=emb_rows[:, j, cols],
                     in0=sines[:, j, cols],
                     scalar=amplitude[:, j : j + 1],
-                    in1=t_all[:, cols],
+                    in1=t_of(c),
                     op0=ALU.mult,
                     op1=ALU.mult,
                 )
 
-        def regroup(c):
-            split = c * CHUNK + VECTOR_COLS
-            for copy, cols in (
-                (nc.vector.tensor_copy, slice(c * CHUNK, split)),
-                (nc.scalar.copy, slice(split, (c + 1) * CHUNK)),
-            ):
-                copy(
-                    out=emb_grouped[:, cols, :].rearrange("p (g i) j -> p g j i", i=RUN),
-                    in_=emb_rows[:, :, cols].rearrange("p j (g i) -> p g j i", i=RUN),
+        def regroup(grouped, by_rows, c, on_gpsimd):
+            cols = slice(c * CHUNK, (c + 1) * CHUNK)
+            if on_gpsimd:
+                nc.gpsimd.tensor_scalar(
+                    out=grouped[:],
+                    in0=by_rows[:, :, cols].rearrange("p j b -> p b j"),
+                    scalar1=1.0,
+                    scalar2=0.0,
+                    op0=ALU.mult,
+                    op1=ALU.add,
+                )
+            else:
+                nc.vector.tensor_copy(
+                    out=grouped[:].rearrange("p (g i) j -> p g j i", i=RUN),
+                    in_=by_rows[:, :, cols].rearrange("p j (g i) -> p g j i", i=RUN),
                 )
 
-        def quantise_emb(c):
+        def regroup_emb(c, on_gpsimd):
+            emb_grouped[c] = keep.tile([P, CHUNK, PACK], BF16, name="emb_grouped", tag="emb_grouped", align_bytes=64)
+            regroup(emb_grouped[c], emb_rows, c, on_gpsimd)
+
+        def regroup_h(c, on_gpsimd):
+            h_grouped[c] = keep.tile([P, CHUNK, PACK], BF16, name="h_grouped", tag="h_grouped", align_bytes=64)
+            regroup(h_grouped[c], h_rows, c, on_gpsimd)
+
+        def sort_w1():
+            nc.vector.tensor_copy(
+                out=w1_codes[:].rearrange("p (j m) -> p j m", j=PACK),
+                in_=w_words[:, 0, :].bitcast(I32).rearrange("p (m j) -> p j m", j=PACK),
+            )
+            nc.vector.tensor_copy(
+                out=w1_scales[:].rearrange("p (j m) -> p m j", j=PACK),
+                in_=w_scales[:, 0, :].rearrange("p (m j) -> p m j", j=PACK),
+            )
+            nc.vector.tensor_copy(out=b1_cols[:], in_=b1_bf[:])
+
+        def quantise(codes, scales, grouped, c):
             cols = slice(c * CHUNK, (c + 1) * CHUNK)
             nc.vector.quantize_mx(
-                out=emb_codes[:, cols].bitcast(FP8X4),
-                scales=emb_scales[:, cols],
-                in_=emb_grouped[:, cols, :].rearrange("p b j -> p (b j)"),
+                out=codes[:, cols].bitcast(FP8X4),
+                scales=scales[:, cols],
+                in_=grouped[:].rearrange("p b j -> p (b j)"),
             )
 
-        def layer1_matmuls(c):
-            for i in blocks_of(c):
-                rows = slice(i * P, (i + 1) * P)
-                acc_1[i] = psum_acc.tile([P, H], F32, name="acc_1", tag="acc")
+        def quantise_emb(c):
+            quantise(emb_codes, emb_scales, emb_grouped[c], c)
+
+        def quantise_h(c):
+            quantise(h_codes, h_scales, h_grouped[c], c)
+
+        def layer1_matmuls(c, tiles):
+            cols = slice(c * CHUNK, (c + 1) * CHUNK)
+            for j in tiles:
+                acc_1[(c, j)] = psum_acc.tile([P, CHUNK], F32, name="acc_1", tag="acc")
                 nc.tensor.matmul_mx(
-                    out=acc_1[i][:],
-                    lhsT=emb_codes[:, rows].bitcast(FP8X4),
-                    lhsT_scale=emb_scales[:, rows],
-                    rhs=w_words[:, 0, :].bitcast(FP8X4),
-                    rhs_scale=w_scales[:, 0, :],
+                    out=acc_1[(c, j)][:],
+                    lhsT=w1_codes[:, j * P : (j + 1) * P].bitcast(FP8X4),
+                    lhsT_scale=w1_scales[:, j * P : (j + 1) * P],
+                    rhs=emb_codes[:, cols].bitcast(FP8X4),
+                    rhs_scale=emb_scales[:, cols],
                     start=True,
                     stop=True,
                 )
 
-        def layer1_bias_and_transpose(c):
-            for i in blocks_of(c):
-                pre_1 = work.tile([P, PACK, P], F32)
-                nc.vector.tensor_tensor(
-                    out=pre_1[:], in0=acc_1[i][:].rearrange("b (p j) -> b j p", j=PACK), in1=b1_sorted[:], op=ALU.add
-                )
-                pre_1T[i] = psum_t.tile([P, PACK, P], F32, name="pre_1T", tag="flipped")
-                for j in range(PACK):
-                    nc.tensor.transpose(pre_1T[i][:, j, :], pre_1[:, j, :], identity[:])
-
         def layer1_silu(c):
-            for i in blocks_of(c):
-                rows = slice(i * P, (i + 1) * P)
+            cols = slice(c * CHUNK, (c + 1) * CHUNK)
+            for j in range(PACK):
                 nc.scalar.activation(
-                    out=h_grouped[:, rows, :], in_=pre_1T[i][:].rearrange("p j b -> p b j"), func=ACT.Silu
+                    out=h_rows[:, j, cols], in_=acc_1[(c, j)][:], func=ACT.Silu, bias=b1_cols[:, j : j + 1]
                 )
 
-        def quantise_h(c):
-            for i in blocks_of(c):
-                rows = slice(i * P, (i + 1) * P)
-                nc.vector.quantize_mx(
-                    out=h_codes[:, rows].bitcast(FP8X4),
-                    scales=h_scales[:, rows],
-                    in_=h_grouped[:, rows, :].rearrange("p b j -> p (b j)"),
-                )
+        def strips_of(c):
+            return range(c * STRIPS_PER_CHUNK, (c + 1) * STRIPS_PER_CHUNK)
 
         def layer2_matmuls(c):
-            for i in blocks_of(c):
-                rows = slice(i * P, (i + 1) * P)
+            for i in strips_of(c):
+                cols = slice(i * P, (i + 1) * P)
                 acc_2[i] = psum_acc.tile([P, O], F32, name="acc_2", tag="acc")
                 nc.tensor.matmul_mx(
                     out=acc_2[i][:],
-                    lhsT=h_codes[:, rows].bitcast(FP8X4),
-                    lhsT_scale=h_scales[:, rows],
+                    lhsT=h_codes[:, cols].bitcast(FP8X4),
+                    lhsT_scale=h_scales[:, cols],
                     rhs=w_words[:, 1, :].bitcast(FP8X4),
                     rhs_scale=w_scales[:, 1, :],
                     start=True,
                     stop=True,
                 )
 
-        def layer2_finish(c):
-            for i in blocks_of(c):
-                rows = slice(i * P, (i + 1) * P)
-                pre_2 = work.tile([P, O], F32)
-                nc.vector.tensor_tensor(out=pre_2[:], in0=acc_2[i][:], in1=b2_all[:], op=ALU.add)
-                result = work.tile([P, O], F32)
-                nc.scalar.activation(out=result[:], in_=pre_2[:], func=ACT.Silu)
-                nc.sync.dma_start(out=out[rows, :], in_=result[:])
+        def layer2_bias(c):
+            for i in strips_of(c):
+                if i % 2 == 0:
+                    pre_2[i // 2] = work.tile([P, 2, O], F32, name="pre_2", tag="pre_2")
+                nc.vector.tensor_tensor(out=pre_2[i // 2][:, i % 2, :], in0=acc_2[i][:], in1=b2_all[:], op=ALU.add)
+
+        def layer2_silu(c):
+            for pair in range(2 * c, 2 * c + 2):
+                result = work.tile([P, 2, O], F32, name="result", tag="result")
+                nc.scalar.activation(out=result[:], in_=pre_2[pair][:], func=ACT.Silu)
+                nc.sync.dma_start(
+                    out=out[pair * 2 * P : (pair + 1) * 2 * P, :].rearrange("(s q) o -> q s o", s=2), in_=result[:]
+                )
 
         for c in range(CHUNKS):
-            put_on_all(c * CHUNK)
+            spread_t(c)
         for c in range(CHUNKS):
             copy_t(c)
-        put_on_all(B)
-        put_on_all(B + H)
-        sines_of(0)
-        sines_of(1)
+        for c in range(CHUNKS):
+            sines_of(c)
         scale_by_t(0)
-        regroup(0)
-        sines_of(2)
+        sort_w1()
+        regroup_emb(0, True)
         scale_by_t(1)
         quantise_emb(0)
-        layer1_matmuls(0)
-        regroup(1)
-        sines_of(3)
-        nc.vector.tensor_copy(out=b1_sorted[:], in_=on_all[B][:].rearrange("b (p j) -> b j p", j=PACK))
-        nc.vector.tensor_copy(out=b2_all[:], in_=on_all[B + H][:])
-        for c in range(CHUNKS + 1):
-            if c < CHUNKS:
-                layer1_bias_and_transpose(c)
-                layer1_silu(c)
-            if c >= 1:
-                quantise_h(c - 1)
-                layer2_matmuls(c - 1)
+        layer1_matmuls(0, (0, 1, 2, 3))
+        regroup_emb(1, True)
+        scale_by_t(2)
+        quantise_emb(1)
+        layer1_matmuls(1, (0, 1))
+        regroup_emb(2, True)
+        scale_by_t(3)
+        quantise_emb(2)
+        regroup_emb(3, False)
+        layer1_silu(0)
+        layer1_matmuls(1, (2, 3))
+        regroup_h(0, False)
+        quantise_emb(3)
+        layer1_silu(1)
+        layer1_matmuls(2, (0, 1, 2, 3))
+        quantise_h(0)
+        layer1_silu(2)
+        layer2_matmuls(0)
+        regroup_h(1, True)
+        layer2_bias(0)
+        layer2_silu(0)
+        layer1_matmuls(3, (0, 1, 2, 3))
+        layer1_silu(3)
+        for c in range(1, CHUNKS):
+            quantise_h(c)
+            layer2_matmuls(c)
             if c + 1 < CHUNKS:
-                quantise_emb(c + 1)
-            if c + 2 < CHUNKS:
-                scale_by_t(c + 2)
-                regroup(c + 2)
-            if c >= 1:
-                layer2_finish(c - 1)
-            if c + 1 < CHUNKS:
-                layer1_matmuls(c + 1)
+                regroup_h(c + 1, True)
+            layer2_bias(c)
+            layer2_silu(c)

@@ -236,9 +236,9 @@ def tile_input_timestep_kernel(tc, t, W1_words, W1_scales, b1, W2_words, W2_scal
         for c in range(CHUNKS):
             sines_of(c)
         scale_by_t(0)
-        sort_w1()
         regroup_emb(0, True)
         scale_by_t(1)
+        sort_w1()
         quantise_emb(0)
         layer1_matmuls(0, (0, 1, 2, 3))
         regroup_emb(1, True)

@@ -27,9 +27,8 @@ def tile_input_timestep_kernel(tc, t, W1_words, W1_scales, b1, W2_words, W2_scal
     nc = tc.nc
     with ExitStack() as ctx:
         keep = ctx.enter_context(tc.tile_pool(name="keep", bufs=1))
-        work = ctx.enter_context(tc.tile_pool(name="work", bufs=3))
-        psum_acc = ctx.enter_context(tc.psum_pool(name="psum_acc", bufs=6))
-        psum_t = ctx.enter_context(tc.psum_pool(name="psum_t", bufs=2))
+        work = ctx.enter_context(tc.tile_pool(name="work", bufs=6))
+        psum = ctx.enter_context(tc.psum_pool(name="psum", bufs=8))
         ctx.enter_context(tc.manual_schedule())
 
         rows = keep.tile([P, B], BF16)
@@ -59,19 +58,15 @@ def tile_input_timestep_kernel(tc, t, W1_words, W1_scales, b1, W2_words, W2_scal
 
         ones = keep.tile([P, P], BF16)
         nc.gpsimd.memset(ones[:], 1.0)
-        t_psum = {}
-        t_all = keep.tile([P, B], BF16)
+        t_scalar = [psum.tile([P, CHUNK], BF16, name="t_scalar", tag="bank") for c in range(CHUNKS)]
+        t_vector = [psum.tile([P, 2 * CHUNK], BF16, name="t_vector", tag="bank") for half in range(CHUNKS // 2)]
 
         def t_of(c):
-            return t_psum[c // 2][:, (c % 2) * CHUNK : (c % 2 + 1) * CHUNK]
+            return t_vector[c // 2][:, (c % 2) * CHUNK : (c % 2 + 1) * CHUNK]
 
         def spread_t(c):
-            if c % 2 == 0:
-                t_psum[c // 2] = psum_t.tile([P, 2 * CHUNK], BF16, name="t_psum", tag="t_psum")
-            nc.tensor.matmul(out=t_of(c), lhsT=ones[:], rhs=rows[:, c * CHUNK : (c + 1) * CHUNK], start=True, stop=True)
-
-        def copy_t(c):
-            nc.vector.tensor_copy(out=t_all[:, c * CHUNK : (c + 1) * CHUNK], in_=t_of(c))
+            for spread in (t_scalar[c][:], t_of(c)):
+                nc.tensor.matmul(out=spread, lhsT=ones[:], rhs=rows[:, c * CHUNK : (c + 1) * CHUNK], start=True, stop=True)
 
         k_int = keep.tile([P, PACK], I32)
         nc.gpsimd.iota(k_int[:], pattern=[[1, PACK]], base=0, channel_multiplier=PACK)
@@ -109,7 +104,7 @@ def tile_input_timestep_kernel(tc, t, W1_words, W1_scales, b1, W2_words, W2_scal
             for j in range(PACK):
                 nc.scalar.activation(
                     out=sines[:, j, cols],
-                    in_=t_all[:, cols],
+                    in_=t_scalar[c][:],
                     func=ACT.Sin,
                     bias=shift[:, j : j + 1],
                     scale=neg_phase[:, j : j + 1],
@@ -127,9 +122,9 @@ def tile_input_timestep_kernel(tc, t, W1_words, W1_scales, b1, W2_words, W2_scal
                     op1=ALU.mult,
                 )
 
-        def regroup(grouped, by_rows, c, on_gpsimd):
+        def regroup(grouped, by_rows, c, engine):
             cols = slice(c * CHUNK, (c + 1) * CHUNK)
-            if on_gpsimd:
+            if engine == "gpsimd":
                 nc.gpsimd.tensor_scalar(
                     out=grouped[:],
                     in0=by_rows[:, :, cols].rearrange("p j b -> p b j"),
@@ -139,18 +134,20 @@ def tile_input_timestep_kernel(tc, t, W1_words, W1_scales, b1, W2_words, W2_scal
                     op1=ALU.add,
                 )
             else:
-                nc.vector.tensor_copy(
+                copy = nc.vector.tensor_copy if engine == "vector" else nc.scalar.copy
+                copy(
                     out=grouped[:].rearrange("p (g i) j -> p g j i", i=RUN),
                     in_=by_rows[:, :, cols].rearrange("p j (g i) -> p g j i", i=RUN),
                 )
 
-        def regroup_emb(c, on_gpsimd):
-            emb_grouped[c] = keep.tile([P, CHUNK, PACK], BF16, name="emb_grouped", tag="emb_grouped", align_bytes=64)
-            regroup(emb_grouped[c], emb_rows, c, on_gpsimd)
+        def regroup_emb(c, engine):
+            tag = "emb_grouped_scalar" if engine == "scalar" else "emb_grouped"
+            emb_grouped[c] = keep.tile([P, CHUNK, PACK], BF16, name="emb_grouped", tag=tag, align_bytes=64)
+            regroup(emb_grouped[c], emb_rows, c, engine)
 
-        def regroup_h(c, on_gpsimd):
+        def regroup_h(c, engine):
             h_grouped[c] = keep.tile([P, CHUNK, PACK], BF16, name="h_grouped", tag="h_grouped", align_bytes=64)
-            regroup(h_grouped[c], h_rows, c, on_gpsimd)
+            regroup(h_grouped[c], h_rows, c, engine)
 
         def sort_w1():
             nc.vector.tensor_copy(
@@ -180,7 +177,7 @@ def tile_input_timestep_kernel(tc, t, W1_words, W1_scales, b1, W2_words, W2_scal
         def layer1_matmuls(c, tiles):
             cols = slice(c * CHUNK, (c + 1) * CHUNK)
             for j in tiles:
-                acc_1[(c, j)] = psum_acc.tile([P, CHUNK], F32, name="acc_1", tag="acc")
+                acc_1[(c, j)] = psum.tile([P, CHUNK], F32, name="acc_1", tag="bank")
                 nc.tensor.matmul_mx(
                     out=acc_1[(c, j)][:],
                     lhsT=w1_codes[:, j * P : (j + 1) * P].bitcast(FP8X4),
@@ -204,7 +201,7 @@ def tile_input_timestep_kernel(tc, t, W1_words, W1_scales, b1, W2_words, W2_scal
         def layer2_matmuls(c):
             for i in strips_of(c):
                 cols = slice(i * P, (i + 1) * P)
-                acc_2[i] = psum_acc.tile([P, O], F32, name="acc_2", tag="acc")
+                acc_2[i] = psum.tile([P, O], F32, name="acc_2", tag="bank")
                 nc.tensor.matmul_mx(
                     out=acc_2[i][:],
                     lhsT=h_codes[:, cols].bitcast(FP8X4),
@@ -215,58 +212,59 @@ def tile_input_timestep_kernel(tc, t, W1_words, W1_scales, b1, W2_words, W2_scal
                     stop=True,
                 )
 
-        def layer2_bias(c):
-            for i in strips_of(c):
+        def layer2_bias(pair):
+            for i in (2 * pair, 2 * pair + 1):
                 if i % 2 == 0:
                     pre_2[i // 2] = work.tile([P, 2, O], F32, name="pre_2", tag="pre_2")
                 nc.vector.tensor_tensor(out=pre_2[i // 2][:, i % 2, :], in0=acc_2[i][:], in1=b2_all[:], op=ALU.add)
 
-        def layer2_silu(c):
-            for pair in range(2 * c, 2 * c + 2):
-                result = work.tile([P, 2, O], F32, name="result", tag="result")
-                nc.scalar.activation(out=result[:], in_=pre_2[pair][:], func=ACT.Silu)
-                nc.sync.dma_start(
-                    out=out[pair * 2 * P : (pair + 1) * 2 * P, :].rearrange("(s q) o -> q s o", s=2), in_=result[:]
-                )
+        def layer2_silu(pair):
+            result = work.tile([P, 2, O], F32, name="result", tag="result")
+            nc.scalar.activation(out=result[:], in_=pre_2[pair][:], func=ACT.Silu)
+            nc.sync.dma_start(
+                out=out[pair * 2 * P : (pair + 1) * 2 * P, :].rearrange("(s q) o -> q s o", s=2), in_=result[:]
+            )
 
         for c in range(CHUNKS):
             spread_t(c)
         for c in range(CHUNKS):
-            copy_t(c)
-        for c in range(CHUNKS):
             sines_of(c)
         scale_by_t(0)
-        regroup_emb(0, True)
+        regroup_emb(0, "gpsimd")
         scale_by_t(1)
         sort_w1()
         quantise_emb(0)
         layer1_matmuls(0, (0, 1, 2, 3))
-        regroup_emb(1, True)
+        regroup_emb(1, "gpsimd")
         scale_by_t(2)
         quantise_emb(1)
-        layer1_matmuls(1, (0, 1))
-        regroup_emb(2, True)
+        layer1_matmuls(1, (0, 1, 2))
+        regroup_emb(2, "gpsimd")
         scale_by_t(3)
+        layer1_matmuls(1, (3,))
         quantise_emb(2)
-        regroup_emb(3, False)
         layer1_silu(0)
-        layer1_matmuls(1, (2, 3))
-        regroup_h(0, False)
+        regroup_emb(3, "scalar")
+        regroup_h(0, "vector")
         quantise_emb(3)
         layer1_silu(1)
         layer1_matmuls(2, (0, 1, 2, 3))
         quantise_h(0)
         layer1_silu(2)
         layer2_matmuls(0)
-        regroup_h(1, True)
+        regroup_h(1, "gpsimd")
         layer2_bias(0)
-        layer2_silu(0)
         layer1_matmuls(3, (0, 1, 2, 3))
         layer1_silu(3)
+        layer2_silu(0)
         for c in range(1, CHUNKS):
             quantise_h(c)
+            layer2_bias(2 * c - 1)
+            layer2_silu(2 * c - 1)
             layer2_matmuls(c)
             if c + 1 < CHUNKS:
-                regroup_h(c + 1, True)
-            layer2_bias(c)
-            layer2_silu(c)
+                regroup_h(c + 1, "gpsimd")
+            layer2_bias(2 * c)
+            layer2_silu(2 * c)
+        layer2_bias(2 * CHUNKS - 1)
+        layer2_silu(2 * CHUNKS - 1)

@@ -18,6 +18,7 @@ B, D, H, O = 2048, 512, 512, 512
 CHUNK = 512
 CHUNKS = B // CHUNK
 STRIPS_PER_CHUNK = CHUNK // P
+PAIRS = B // (2 * P)
 RUN = 4
 
 FLOPS = 2 * B * (D * H + H * O)
@@ -66,7 +67,13 @@ def tile_input_timestep_kernel(tc, t, W1_words, W1_scales, b1, W2_words, W2_scal
 
         def spread_t(c):
             for spread in (t_scalar[c][:], t_of(c)):
-                nc.tensor.matmul(out=spread, lhsT=ones[:], rhs=rows[:, c * CHUNK : (c + 1) * CHUNK], start=True, stop=True)
+                nc.tensor.matmul(
+                    out=spread.rearrange("p (k s q) -> p k s q", k=2, s=2),
+                    lhsT=ones[:],
+                    rhs=rows[:, c * CHUNK : (c + 1) * CHUNK].rearrange("p (k q s) -> p k s q", k=2, s=2),
+                    start=True,
+                    stop=True,
+                )
 
         k_int = keep.tile([P, PACK], I32)
         nc.gpsimd.iota(k_int[:], pattern=[[1, PACK]], base=0, channel_multiplier=PACK)
@@ -98,6 +105,7 @@ def tile_input_timestep_kernel(tc, t, W1_words, W1_scales, b1, W2_words, W2_scal
         acc_1 = {}
         acc_2 = {}
         pre_2 = {}
+        out_by_pair = out.rearrange("(k q s) o -> k q s o", k=PAIRS, s=2)
 
         def sines_of(c):
             cols = slice(c * CHUNK, (c + 1) * CHUNK)
@@ -221,9 +229,7 @@ def tile_input_timestep_kernel(tc, t, W1_words, W1_scales, b1, W2_words, W2_scal
         def layer2_silu(pair):
             result = work.tile([P, 2, O], F32, name="result", tag="result")
             nc.scalar.activation(out=result[:], in_=pre_2[pair][:], func=ACT.Silu)
-            nc.sync.dma_start(
-                out=out[pair * 2 * P : (pair + 1) * 2 * P, :].rearrange("(s q) o -> q s o", s=2), in_=result[:]
-            )
+            nc.sync.dma_start(out=out_by_pair[pair], in_=result[:])
 
         for c in range(CHUNKS):
             spread_t(c)

@@ -20,6 +20,7 @@ CHUNKS = B // CHUNK
 STRIPS_PER_CHUNK = CHUNK // P
 PAIRS = B // (2 * P)
 RUN = 4
+STRIPWISE_PAIRS = 3
 
 FLOPS = 2 * B * (D * H + H * O)
 
@@ -220,16 +221,25 @@ def tile_input_timestep_kernel(tc, t, W1_words, W1_scales, b1, W2_words, W2_scal
                     stop=True,
                 )
 
-        def layer2_bias(pair):
-            for i in (2 * pair, 2 * pair + 1):
-                if i % 2 == 0:
-                    pre_2[i // 2] = work.tile([P, 2, O], F32, name="pre_2", tag="pre_2")
-                nc.vector.tensor_tensor(out=pre_2[i // 2][:, i % 2, :], in0=acc_2[i][:], in1=b2_all[:], op=ALU.add)
+        def layer2_bias(i):
+            if i % 2 == 0:
+                pre_2[i // 2] = work.tile([P, 2, O], F32, name="pre_2", tag="pre_2")
+            nc.vector.tensor_tensor(out=pre_2[i // 2][:, i % 2, :], in0=acc_2[i][:], in1=b2_all[:], op=ALU.add)
 
-        def layer2_silu(pair):
+        def layer2_silu(pair, strips):
             result = work.tile([P, 2, O], F32, name="result", tag="result")
-            nc.scalar.activation(out=result[:], in_=pre_2[pair][:], func=ACT.Silu)
-            nc.sync.dma_start(out=out_by_pair[pair], in_=result[:])
+            nc.scalar.activation(out=result[:, strips, :], in_=pre_2[pair][:, strips, :], func=ACT.Silu)
+            nc.sync.dma_start(out=out_by_pair[pair][:, strips, :], in_=result[:, strips, :])
+
+        def layer2_finish(pair):
+            if pair < PAIRS - STRIPWISE_PAIRS:
+                layer2_bias(2 * pair)
+                layer2_bias(2 * pair + 1)
+                layer2_silu(pair, slice(0, 2))
+            else:
+                for s in range(2):
+                    layer2_bias(2 * pair + s)
+                    layer2_silu(pair, slice(s, s + 1))
 
         for c in range(CHUNKS):
             spread_t(c)
@@ -260,17 +270,15 @@ def tile_input_timestep_kernel(tc, t, W1_words, W1_scales, b1, W2_words, W2_scal
         layer2_matmuls(0)
         regroup_h(1, "gpsimd")
         layer2_bias(0)
+        layer2_bias(1)
         layer1_matmuls(3, (0, 1, 2, 3))
         layer1_silu(3)
-        layer2_silu(0)
+        layer2_silu(0, slice(0, 2))
         for c in range(1, CHUNKS):
             quantise_h(c)
-            layer2_bias(2 * c - 1)
-            layer2_silu(2 * c - 1)
+            layer2_finish(2 * c - 1)
             layer2_matmuls(c)
             if c + 1 < CHUNKS:
                 regroup_h(c + 1, "gpsimd")
-            layer2_bias(2 * c)
-            layer2_silu(2 * c)
-        layer2_bias(2 * CHUNKS - 1)
-        layer2_silu(2 * CHUNKS - 1)
+            layer2_finish(2 * c)
+        layer2_finish(PAIRS - 1)

@@ -231,15 +231,13 @@ def tile_input_timestep_kernel(tc, t, W1_words, W1_scales, b1, W2_words, W2_scal
             nc.scalar.activation(out=result[:, strips, :], in_=pre_2[pair][:, strips, :], func=ACT.Silu)
             nc.sync.dma_start(out=out_by_pair[pair][:, strips, :], in_=result[:, strips, :])
 
-        def layer2_finish(pair):
-            if pair < PAIRS - STRIPWISE_PAIRS:
-                layer2_bias(2 * pair)
-                layer2_bias(2 * pair + 1)
-                layer2_silu(pair, slice(0, 2))
-            else:
-                for s in range(2):
-                    layer2_bias(2 * pair + s)
-                    layer2_silu(pair, slice(s, s + 1))
+        def layer2_finish(strips):
+            for i in strips:
+                layer2_bias(i)
+                if i // 2 >= PAIRS - STRIPWISE_PAIRS:
+                    layer2_silu(i // 2, slice(i % 2, i % 2 + 1))
+                elif i % 2 == 1:
+                    layer2_silu(i // 2, slice(0, 2))
 
         for c in range(CHUNKS):
             spread_t(c)
@@ -269,16 +267,15 @@ def tile_input_timestep_kernel(tc, t, W1_words, W1_scales, b1, W2_words, W2_scal
         layer1_silu(2)
         layer2_matmuls(0)
         regroup_h(1, "gpsimd")
-        layer2_bias(0)
-        layer2_bias(1)
+        layer2_finish((0, 1, 2, 3))
         layer1_matmuls(3, (0, 1, 2, 3))
         layer1_silu(3)
-        layer2_silu(0, slice(0, 2))
         for c in range(1, CHUNKS):
             quantise_h(c)
-            layer2_finish(2 * c - 1)
+            if c > 1:
+                layer2_finish((4 * c - 1,))
             layer2_matmuls(c)
             if c + 1 < CHUNKS:
                 regroup_h(c + 1, "gpsimd")
-            layer2_finish(2 * c)
-        layer2_finish(PAIRS - 1)
+            layer2_finish((4 * c, 4 * c + 1, 4 * c + 2))
+        layer2_finish((4 * CHUNKS - 1,))

@@ -20,6 +20,7 @@ CHUNKS = B // CHUNK
 STRIPS_PER_CHUNK = CHUNK // P
 PAIRS = B // (2 * P)
 RUN = 4
+SCALAR_COLS = 384
 STRIPWISE_PAIRS = 3
 
 FLOPS = 2 * B * (D * H + H * O)
@@ -131,11 +132,12 @@ def tile_input_timestep_kernel(tc, t, W1_words, W1_scales, b1, W2_words, W2_scal
                     op1=ALU.mult,
                 )
 
-        def regroup(grouped, by_rows, c, engine):
-            cols = slice(c * CHUNK, (c + 1) * CHUNK)
+        def regroup(grouped, by_rows, c, engine, first=0, last=CHUNK):
+            cols = slice(c * CHUNK + first, c * CHUNK + last)
+            grouped = grouped[:, first:last, :]
             if engine == "gpsimd":
                 nc.gpsimd.tensor_scalar(
-                    out=grouped[:],
+                    out=grouped,
                     in0=by_rows[:, :, cols].rearrange("p j b -> p b j"),
                     scalar1=1.0,
                     scalar2=0.0,
@@ -145,14 +147,14 @@ def tile_input_timestep_kernel(tc, t, W1_words, W1_scales, b1, W2_words, W2_scal
             else:
                 copy = nc.vector.tensor_copy if engine == "vector" else nc.scalar.copy
                 copy(
-                    out=grouped[:].rearrange("p (g i) j -> p g j i", i=RUN),
+                    out=grouped.rearrange("p (g i) j -> p g j i", i=RUN),
                     in_=by_rows[:, :, cols].rearrange("p j (g i) -> p g j i", i=RUN),
                 )
 
         def regroup_emb(c, engine):
             tag = "emb_grouped_scalar" if engine == "scalar" else "emb_grouped"
             emb_grouped[c] = keep.tile([P, CHUNK, PACK], BF16, name="emb_grouped", tag=tag, align_bytes=64)
-            regroup(emb_grouped[c], emb_rows, c, engine)
+            regroup(emb_grouped[c], emb_rows, c, engine, 0, SCALAR_COLS if engine == "scalar" else CHUNK)
 
         def regroup_h(c, engine):
             h_grouped[c] = keep.tile([P, CHUNK, PACK], BF16, name="h_grouped", tag="h_grouped", align_bytes=64)
@@ -260,10 +262,11 @@ def tile_input_timestep_kernel(tc, t, W1_words, W1_scales, b1, W2_words, W2_scal
         layer1_silu(0)
         regroup_emb(3, "scalar")
         regroup_h(0, "vector")
+        regroup(emb_grouped[3], emb_rows, 3, "vector", SCALAR_COLS, CHUNK)
+        quantise_h(0)
         quantise_emb(3)
         layer1_silu(1)
         layer1_matmuls(2, (0, 1, 2, 3))
-        quantise_h(0)
         layer1_silu(2)
         layer2_matmuls(0)
         regroup_h(1, "gpsimd")

@@ -60,7 +60,7 @@ def tile_input_timestep_kernel(tc, t, W1_words, W1_scales, b1, W2_words, W2_scal
         nc.sync.dma_start(out=b2_all[:], in_=b2.partition_broadcast(P))
 
         ones = keep.tile([P, P], BF16)
-        nc.gpsimd.memset(ones[:], 1.0)
+        nc.vector.memset(ones[:], 1.0)
         t_scalar = [psum.tile([P, CHUNK], BF16, name="t_scalar", tag="bank") for c in range(CHUNKS)]
         t_vector = [psum.tile([P, 2 * CHUNK], BF16, name="t_vector", tag="bank") for half in range(CHUNKS // 2)]
 

@@ -34,6 +34,11 @@ def tile_input_timestep_kernel(tc, t, W1_words, W1_scales, b1, W2_words, W2_scal
         psum = ctx.enter_context(tc.psum_pool(name="psum", bufs=8))
         ctx.enter_context(tc.manual_schedule())
 
+        silu_seed = keep.tile([P, 1], F32)
+        nc.gpsimd.memset(silu_seed[:], 0.0)
+        silu_first = keep.tile([P, 1], F32)
+        nc.scalar.activation(out=silu_first[:], in_=silu_seed[:], func=ACT.Silu)
+
         rows = keep.tile([P, B], BF16)
         for c in range(CHUNKS):
             cols = slice(c * CHUNK, (c + 1) * CHUNK)

@@ -20,7 +20,6 @@ CHUNKS = B // CHUNK
 STRIPS_PER_CHUNK = CHUNK // P
 PAIRS = B // (2 * P)
 RUN = 4
-SCALAR_COLS = 384
 STRIPWISE_PAIRS = 3
 
 FLOPS = 2 * B * (D * H + H * O)
@@ -137,12 +136,11 @@ def tile_input_timestep_kernel(tc, t, W1_words, W1_scales, b1, W2_words, W2_scal
                     op1=ALU.mult,
                 )
 
-        def regroup(grouped, by_rows, c, engine, first=0, last=CHUNK):
-            cols = slice(c * CHUNK + first, c * CHUNK + last)
-            grouped = grouped[:, first:last, :]
+        def regroup(grouped, by_rows, c, engine):
+            cols = slice(c * CHUNK, (c + 1) * CHUNK)
             if engine == "gpsimd":
                 nc.gpsimd.tensor_scalar(
-                    out=grouped,
+                    out=grouped[:],
                     in0=by_rows[:, :, cols].rearrange("p j b -> p b j"),
                     scalar1=1.0,
                     scalar2=0.0,
@@ -152,17 +150,17 @@ def tile_input_timestep_kernel(tc, t, W1_words, W1_scales, b1, W2_words, W2_scal
             else:
                 copy = nc.vector.tensor_copy if engine == "vector" else nc.scalar.copy
                 copy(
-                    out=grouped.rearrange("p (g i) j -> p g j i", i=RUN),
+                    out=grouped[:].rearrange("p (g i) j -> p g j i", i=RUN),
                     in_=by_rows[:, :, cols].rearrange("p j (g i) -> p g j i", i=RUN),
                 )
 
         def regroup_emb(c, engine):
-            tag = "emb_grouped_scalar" if engine == "scalar" else "emb_grouped"
-            emb_grouped[c] = keep.tile([P, CHUNK, PACK], BF16, name="emb_grouped", tag=tag, align_bytes=64)
-            regroup(emb_grouped[c], emb_rows, c, engine, 0, SCALAR_COLS if engine == "scalar" else CHUNK)
+            emb_grouped[c] = keep.tile([P, CHUNK, PACK], BF16, name="emb_grouped", tag="emb_grouped", align_bytes=64)
+            regroup(emb_grouped[c], emb_rows, c, engine)
 
         def regroup_h(c, engine):
-            h_grouped[c] = keep.tile([P, CHUNK, PACK], BF16, name="h_grouped", tag="h_grouped", align_bytes=64)
+            tag = "h_grouped_scalar" if engine == "scalar" else "h_grouped"
+            h_grouped[c] = keep.tile([P, CHUNK, PACK], BF16, name="h_grouped", tag=tag, align_bytes=64)
             regroup(h_grouped[c], h_rows, c, engine)
 
         def sort_w1():
@@ -262,28 +260,29 @@ def tile_input_timestep_kernel(tc, t, W1_words, W1_scales, b1, W2_words, W2_scal
         layer1_matmuls(1, (0, 1, 2))
         regroup_emb(2, "gpsimd")
         scale_by_t(3)
+        layer1_silu(0)
         layer1_matmuls(1, (3,))
         quantise_emb(2)
-        layer1_silu(0)
-        regroup_emb(3, "scalar")
-        regroup_h(0, "vector")
-        regroup(emb_grouped[3], emb_rows, 3, "vector", SCALAR_COLS, CHUNK)
-        quantise_h(0)
-        quantise_emb(3)
+        regroup_h(0, "scalar")
         layer1_silu(1)
         layer1_matmuls(2, (0, 1, 2, 3))
+        quantise_h(0)
+        regroup_emb(3, "vector")
         layer1_silu(2)
         layer2_matmuls(0)
-        regroup_h(1, "gpsimd")
-        layer2_finish((0, 1, 2, 3))
+        quantise_emb(3)
         layer1_matmuls(3, (0, 1, 2, 3))
+        regroup_h(1, "vector")
         layer1_silu(3)
-        for c in range(1, CHUNKS):
-            quantise_h(c)
-            if c > 1:
-                layer2_finish((4 * c - 1,))
-            layer2_matmuls(c)
-            if c + 1 < CHUNKS:
-                regroup_h(c + 1, "gpsimd")
-            layer2_finish((4 * c, 4 * c + 1, 4 * c + 2))
-        layer2_finish((4 * CHUNKS - 1,))
+        layer2_finish((0,))
+        quantise_h(1)
+        layer2_matmuls(1)
+        regroup_h(2, "gpsimd")
+        layer2_finish((1, 2, 3, 4, 5))
+        quantise_h(2)
+        layer2_matmuls(2)
+        regroup_h(3, "gpsimd")
+        layer2_finish((6, 7, 8, 9, 10))
+        quantise_h(3)
+        layer2_matmuls(3)
+        layer2_finish((11, 12, 13, 14, 15))

@@ -39,28 +39,35 @@ def tile_input_timestep_kernel(tc, t, W1_words, W1_scales, b1, W2_words, W2_scal
         nc.scalar.activation(out=silu_first[:], in_=silu_seed[:], func=ACT.Silu)
 
         rows = keep.tile([P, B], BF16)
-        for c in range(CHUNKS):
+
+        def load_t(c):
             cols = slice(c * CHUNK, (c + 1) * CHUNK)
             nc.vector.memset(rows[:, cols].bitcast(I32), 0)
             nc.sync.dma_start(out=rows[0:1, cols], in_=t[cols].unsqueeze(0))
 
         w_scales = keep.tile([P, 2, H], U8, align_bytes=64)
-        nc.vector.memset(w_scales[:].rearrange("p w n -> p (w n)").bitcast(I32), 0)
         w_words = keep.tile([P, 2, PACK * H], U8, align_bytes=64)
         b1_bf = keep.tile([P, PACK], BF16)
         b2_all = keep.tile([P, O], BF16)
-        for w, (words, scales) in enumerate(((W1_words, W1_scales), (W2_words, W2_scales))):
+
+        def load_weight(w, words, scales):
+            nc.sync.dma_start(
+                out=w_words[:, w, :].bitcast(I32),
+                in_=words[0].rearrange("p n j -> p (n j)").bitcast(I32),
+            )
             for q in range(4):
                 nc.sync.dma_start(
                     out=w_scales[32 * q : 32 * q + 4, w, :].bitcast(I32),
                     in_=scales[0, 4 * q : 4 * q + 4, :].bitcast(I32),
                 )
-            nc.sync.dma_start(
-                out=w_words[:, w, :].bitcast(I32),
-                in_=words[0].rearrange("p n j -> p (n j)").bitcast(I32),
-            )
-            if w == 0:
-                nc.sync.dma_start(out=b1_bf[:], in_=b1.rearrange("(p j) -> p j", j=PACK))
+
+        load_t(0)
+        nc.vector.memset(w_scales[:].rearrange("p w n -> p (w n)").bitcast(I32), 0)
+        load_weight(0, W1_words, W1_scales)
+        nc.sync.dma_start(out=b1_bf[:], in_=b1.rearrange("(p j) -> p j", j=PACK))
+        for c in range(1, CHUNKS):
+            load_t(c)
+        load_weight(1, W2_words, W2_scales)
         nc.sync.dma_start(out=b2_all[:], in_=b2.partition_broadcast(P))
 
         ones = keep.tile([P, P], BF16)
@@ -248,10 +255,10 @@ def tile_input_timestep_kernel(tc, t, W1_words, W1_scales, b1, W2_words, W2_scal
             spread_t(c)
         for c in range(CHUNKS):
             sines_of(c)
+        sort_w1()
         scale_by_t(0)
         regroup_emb(0, "gpsimd")
         scale_by_t(1)
-        sort_w1()
         quantise_emb(0)
         layer1_matmuls(0, (0, 1, 2, 3))
         regroup_emb(1, "gpsimd")

import math
from contextlib import ExitStack

import concourse.mybir as mybir

F32 = mybir.dt.float32
BF16 = mybir.dt.bfloat16
I32 = mybir.dt.int32
U32 = mybir.dt.uint32
U8 = mybir.dt.uint8
FP8X4 = mybir.dt.float8_e4m3fn_x4
ACT = mybir.ActivationFunctionType
ALU = mybir.AluOpType

P = 128
PACK = 4
B, D, H, O = 2048, 512, 512, 512
CHUNK = 512
CHUNKS = B // CHUNK
STRIPS_PER_CHUNK = CHUNK // P
PAIRS = B // (2 * P)
RUN = 4
STRIPWISE_PAIRS = 3

FLOPS = 2 * B * (D * H + H * O)


def tile_input_timestep_kernel(tc, t, W1_words, W1_scales, b1, W2_words, W2_scales, b2, out):
    nc = tc.nc
    with ExitStack() as ctx:
        keep = ctx.enter_context(tc.tile_pool(name="keep", bufs=1))
        work = ctx.enter_context(tc.tile_pool(name="work", bufs=6))
        psum = ctx.enter_context(tc.psum_pool(name="psum", bufs=8))
        ctx.enter_context(tc.manual_schedule())

        silu_seed = keep.tile([P, 1], F32)
        nc.gpsimd.memset(silu_seed[:], 0.0)
        silu_first = keep.tile([P, 1], F32)
        nc.scalar.activation(out=silu_first[:], in_=silu_seed[:], func=ACT.Silu)

        rows = keep.tile([P, B], BF16)

        def load_t(c):
            cols = slice(c * CHUNK, (c + 1) * CHUNK)
            nc.vector.memset(rows[:, cols].bitcast(I32), 0)
            nc.sync.dma_start(out=rows[0:1, cols], in_=t[cols].unsqueeze(0))

        w_scales = keep.tile([P, 2, H], U8, align_bytes=64)
        w_words = keep.tile([P, 2, PACK * H], U8, align_bytes=64)
        b1_bf = keep.tile([P, PACK], BF16)
        b2_all = keep.tile([P, O], BF16)

        def load_weight(w, words, scales):
            nc.sync.dma_start(
                out=w_words[:, w, :].bitcast(I32),
                in_=words[0].rearrange("p n j -> p (n j)").bitcast(I32),
            )
            for q in range(4):
                nc.sync.dma_start(
                    out=w_scales[32 * q : 32 * q + 4, w, :].bitcast(I32),
                    in_=scales[0, 4 * q : 4 * q + 4, :].bitcast(I32),
                )

        load_t(0)
        nc.vector.memset(w_scales[:].rearrange("p w n -> p (w n)").bitcast(I32), 0)
        load_weight(0, W1_words, W1_scales)
        nc.sync.dma_start(out=b1_bf[:], in_=b1.rearrange("(p j) -> p j", j=PACK))
        for c in range(1, CHUNKS):
            load_t(c)
        load_weight(1, W2_words, W2_scales)
        nc.sync.dma_start(out=b2_all[:], in_=b2.partition_broadcast(P))

        ones = keep.tile([P, P], BF16)
        nc.vector.memset(ones[:], 1.0)
        t_scalar = [psum.tile([P, CHUNK], BF16, name="t_scalar", tag="bank") for c in range(CHUNKS)]
        t_vector = [psum.tile([P, 2 * CHUNK], BF16, name="t_vector", tag="bank") for half in range(CHUNKS // 2)]

        def t_of(c):
            return t_vector[c // 2][:, (c % 2) * CHUNK : (c % 2 + 1) * CHUNK]

        def spread_t(c):
            for spread in (t_scalar[c][:], t_of(c)):
                nc.tensor.matmul(
                    out=spread.rearrange("p (k s q) -> p k s q", k=2, s=2),
                    lhsT=ones[:],
                    rhs=rows[:, c * CHUNK : (c + 1) * CHUNK].rearrange("p (k q s) -> p k s q", k=2, s=2),
                    start=True,
                    stop=True,
                )

        k_int = keep.tile([P, PACK], I32)
        nc.gpsimd.iota(k_int[:], pattern=[[1, PACK]], base=0, channel_multiplier=PACK)
        k_f32 = keep.tile([P, PACK], F32)
        nc.vector.tensor_copy(out=k_f32[:], in_=k_int[:])
        neg_phase = keep.tile([P, PACK], F32)
        nc.vector.tensor_scalar(out=neg_phase[:], in0=k_f32[:], scalar1=-math.pi / D, scalar2=None, op0=ALU.mult)
        shift = keep.tile([P, PACK], F32)
        nc.vector.tensor_scalar(
            out=shift[:], in0=k_f32[:], scalar1=math.pi / (2 * D), scalar2=math.pi / 4, op0=ALU.mult, op1=ALU.add
        )
        sin_shift = keep.tile([P, PACK], F32)
        nc.scalar.activation(out=sin_shift[:], in_=shift[:], func=ACT.Sin)
        amplitude = keep.tile([P, PACK], F32)
        nc.vector.tensor_scalar(out=amplitude[:], in0=sin_shift[:], scalar1=2.0, scalar2=None, op0=ALU.mult)

        sines = keep.tile([P, PACK, B], F32)
        emb_rows = keep.tile([P, PACK, B], BF16)
        emb_grouped = {}
        emb_codes = keep.tile([P, B], U32, align_bytes=64)
        emb_scales = keep.tile([P, B], U8, align_bytes=64)
        w1_codes = keep.tile([P, H], I32, align_bytes=64)
        w1_scales = keep.tile([P, H], U8, align_bytes=64)
        b1_cols = keep.tile([P, PACK], F32)
        h_rows = keep.tile([P, PACK, B], BF16)
        h_grouped = {}
        h_codes = keep.tile([P, B], U32, align_bytes=64)
        h_scales = keep.tile([P, B], U8, align_bytes=64)
        acc_1 = {}
        acc_2 = {}
        pre_2 = {}
        out_by_pair = out.rearrange("(k q s) o -> k q s o", k=PAIRS, s=2)

        def sines_of(c):
            cols = slice(c * CHUNK, (c + 1) * CHUNK)
            for j in range(PACK):
                nc.scalar.activation(
                    out=sines[:, j, cols],
                    in_=t_scalar[c][:],
                    func=ACT.Sin,
                    bias=shift[:, j : j + 1],
                    scale=neg_phase[:, j : j + 1],
                )

        def scale_by_t(c):
            cols = slice(c * CHUNK, (c + 1) * CHUNK)
            for j in range(PACK):
                nc.vector.scalar_tensor_tensor(
                    out=emb_rows[:, j, cols],
                    in0=sines[:, j, cols],
                    scalar=amplitude[:, j : j + 1],
                    in1=t_of(c),
                    op0=ALU.mult,
                    op1=ALU.mult,
                )

        def regroup(grouped, by_rows, c, engine):
            cols = slice(c * CHUNK, (c + 1) * CHUNK)
            if engine == "gpsimd":
                nc.gpsimd.tensor_scalar(
                    out=grouped[:],
                    in0=by_rows[:, :, cols].rearrange("p j b -> p b j"),
                    scalar1=1.0,
                    scalar2=0.0,
                    op0=ALU.mult,
                    op1=ALU.add,
                )
            else:
                copy = nc.vector.tensor_copy if engine == "vector" else nc.scalar.copy
                copy(
                    out=grouped[:].rearrange("p (g i) j -> p g j i", i=RUN),
                    in_=by_rows[:, :, cols].rearrange("p j (g i) -> p g j i", i=RUN),
                )

        def regroup_emb(c, engine):
            emb_grouped[c] = keep.tile([P, CHUNK, PACK], BF16, name="emb_grouped", tag="emb_grouped", align_bytes=64)
            regroup(emb_grouped[c], emb_rows, c, engine)

        def regroup_h(c, engine):
            tag = "h_grouped_scalar" if engine == "scalar" else "h_grouped"
            h_grouped[c] = keep.tile([P, CHUNK, PACK], BF16, name="h_grouped", tag=tag, align_bytes=64)
            regroup(h_grouped[c], h_rows, c, engine)

        def sort_w1():
            nc.vector.tensor_copy(
                out=w1_codes[:].rearrange("p (j m) -> p j m", j=PACK),
                in_=w_words[:, 0, :].bitcast(I32).rearrange("p (m j) -> p j m", j=PACK),
            )
            nc.vector.tensor_copy(
                out=w1_scales[:].rearrange("p (j m) -> p m j", j=PACK),
                in_=w_scales[:, 0, :].rearrange("p (m j) -> p m j", j=PACK),
            )
            nc.vector.tensor_copy(out=b1_cols[:], in_=b1_bf[:])

        def quantise(codes, scales, grouped, c):
            cols = slice(c * CHUNK, (c + 1) * CHUNK)
            nc.vector.quantize_mx(
                out=codes[:, cols].bitcast(FP8X4),
                scales=scales[:, cols],
                in_=grouped[:].rearrange("p b j -> p (b j)"),
            )

        def quantise_emb(c):
            quantise(emb_codes, emb_scales, emb_grouped[c], c)

        def quantise_h(c):
            quantise(h_codes, h_scales, h_grouped[c], c)

        def layer1_matmuls(c, tiles):
            cols = slice(c * CHUNK, (c + 1) * CHUNK)
            for j in tiles:
                acc_1[(c, j)] = psum.tile([P, CHUNK], F32, name="acc_1", tag="bank")
                nc.tensor.matmul_mx(
                    out=acc_1[(c, j)][:],
                    lhsT=w1_codes[:, j * P : (j + 1) * P].bitcast(FP8X4),
                    lhsT_scale=w1_scales[:, j * P : (j + 1) * P],
                    rhs=emb_codes[:, cols].bitcast(FP8X4),
                    rhs_scale=emb_scales[:, cols],
                    start=True,
                    stop=True,
                )

        def layer1_silu(c):
            cols = slice(c * CHUNK, (c + 1) * CHUNK)
            for j in range(PACK):
                nc.scalar.activation(
                    out=h_rows[:, j, cols], in_=acc_1[(c, j)][:], func=ACT.Silu, bias=b1_cols[:, j : j + 1]
                )

        def strips_of(c):
            return range(c * STRIPS_PER_CHUNK, (c + 1) * STRIPS_PER_CHUNK)

        def layer2_matmuls(c):
            for i in strips_of(c):
                cols = slice(i * P, (i + 1) * P)
                acc_2[i] = psum.tile([P, O], F32, name="acc_2", tag="bank")
                nc.tensor.matmul_mx(
                    out=acc_2[i][:],
                    lhsT=h_codes[:, cols].bitcast(FP8X4),
                    lhsT_scale=h_scales[:, cols],
                    rhs=w_words[:, 1, :].bitcast(FP8X4),
                    rhs_scale=w_scales[:, 1, :],
                    start=True,
                    stop=True,
                )

        def layer2_bias(i):
            if i % 2 == 0:
                pre_2[i // 2] = work.tile([P, 2, O], F32, name="pre_2", tag="pre_2")
            nc.vector.tensor_tensor(out=pre_2[i // 2][:, i % 2, :], in0=acc_2[i][:], in1=b2_all[:], op=ALU.add)

        def layer2_silu(pair, strips):
            result = work.tile([P, 2, O], F32, name="result", tag="result")
            nc.scalar.activation(out=result[:, strips, :], in_=pre_2[pair][:, strips, :], func=ACT.Silu)
            nc.sync.dma_start(out=out_by_pair[pair][:, strips, :], in_=result[:, strips, :])

        def layer2_finish(strips):
            for i in strips:
                layer2_bias(i)
                if i // 2 >= PAIRS - STRIPWISE_PAIRS:
                    layer2_silu(i // 2, slice(i % 2, i % 2 + 1))
                elif i % 2 == 1:
                    layer2_silu(i // 2, slice(0, 2))

        for c in range(CHUNKS):
            spread_t(c)
        for c in range(CHUNKS):
            sines_of(c)
        sort_w1()
        scale_by_t(0)
        regroup_emb(0, "gpsimd")
        scale_by_t(1)
        quantise_emb(0)
        layer1_matmuls(0, (0, 1, 2, 3))
        regroup_emb(1, "gpsimd")
        scale_by_t(2)
        quantise_emb(1)
        layer1_matmuls(1, (0, 1, 2))
        regroup_emb(2, "gpsimd")
        scale_by_t(3)
        layer1_silu(0)
        layer1_matmuls(1, (3,))
        quantise_emb(2)
        regroup_h(0, "scalar")
        layer1_silu(1)
        layer1_matmuls(2, (0, 1, 2, 3))
        quantise_h(0)
        regroup_emb(3, "vector")
        layer1_silu(2)
        layer2_matmuls(0)
        quantise_emb(3)
        layer1_matmuls(3, (0, 1, 2, 3))
        regroup_h(1, "vector")
        layer1_silu(3)
        layer2_finish((0,))
        quantise_h(1)
        layer2_matmuls(1)
        regroup_h(2, "gpsimd")
        layer2_finish((1, 2, 3, 4, 5))
        quantise_h(2)
        layer2_matmuls(2)
        regroup_h(3, "gpsimd")
        layer2_finish((6, 7, 8, 9, 10))
        quantise_h(3)
        layer2_matmuls(3)
        layer2_finish((11, 12, 13, 14, 15))
